import numpy as np
import ml_dtypes


def mxq(x, axis, fmt="e4m3"):
    dtype, down = {"e4m3": (ml_dtypes.float8_e4m3fn, 7), "e5m2": (ml_dtypes.float8_e5m2, 14)}[fmt]
    v = np.moveaxis(np.asarray(x, np.float32).astype(ml_dtypes.bfloat16).astype(np.float64), axis, -1)
    blocks = v.reshape(v.shape[:-1] + (-1, 32))
    amax = np.abs(blocks).max(-1, keepdims=True)
    byte = np.maximum(np.where(amax > 0, np.frexp(amax)[1] - 1 + 127, 0) - down, 1)
    scale = np.exp2(byte - 127.0)
    codes = (blocks / scale).astype(np.float32).astype(dtype).astype(np.float64)
    return np.moveaxis((codes * scale).reshape(v.shape), -1, axis)


WIDE = False


def mx_kscale(k):
    if not WIDE:
        return np.ones(k)
    levels = np.array([10, -10, 5, -5, 0])
    a = np.random.permutation(np.resize(levels, k // 512 * 4)).reshape(k // 512, 4)
    idx = np.arange(k)
    return np.exp2(a[idx // 512, idx % 128 // 32])


BF16 = ml_dtypes.bfloat16


def bf(x):
    return np.asarray(x, np.float32).astype(BF16)


def f64(x):
    return np.asarray(x).astype(np.float64)


B, T, D, O = 512, 32, 512, 128


def erf(z):
    a = np.clip(z, -6.0, 6.0)
    q = 2.0 * a * a
    term = a.copy()
    total = a.copy()
    for k in range(1, 130):
        term = term * q / (2 * k + 1)
        total = total + term
    return 2.0 / np.sqrt(np.pi) * np.exp(-a * a) * total


def gelu_exact(v):
    return 0.5 * v * (1.0 + erf(v / np.sqrt(2.0)))


def setup_inputs():
    s = mx_kscale(D)
    x = np.random.standard_normal((B, T, D)) * s
    lengths = np.random.randint(T // 4, T + 1, size=B)
    lengths[np.random.randint(B)] = T
    pad = np.arange(T)[None, :] >= lengths[:, None]
    x = np.where(pad[:, :, None], -1.0, x)
    return {"x": bf(x), "W": bf(np.random.standard_normal((O, D)) / np.sqrt(D) / s[None, :]), "b": bf(np.random.standard_normal(O) * 0.3)}


def reference(x, W, b):
    x = f64(x)
    valid = ~np.all(x == -1.0, axis=-1)
    y = gelu_exact((mxq(x, 2, "e4m3") @ mxq(f64(W), 1, "e4m3").T) + f64(b))
    vf = valid[..., None].astype(np.float64)
    n = np.sum(vf, axis=1)
    mean = np.sum(y * vf, axis=1) / n
    diff = (y - mean[:, None, :]) * vf
    var = np.sum(diff * diff, axis=1) / np.maximum(n - 1.0, 1.0)
    std = np.where(n > 1.0, np.sqrt(var), np.zeros_like(var))
    out = np.concatenate([std, mean], axis=-1)
    return np.where(np.isnan(out), np.zeros_like(out), out)

@@ -1,0 +1,184 @@
+import concourse.mybir as mybir
+from concourse.masks import make_identity
+
+F32 = mybir.dt.float32
+BF16 = mybir.dt.bfloat16
+U32 = mybir.dt.uint32
+U8 = mybir.dt.uint8
+FP8X4 = mybir.dt.float8_e4m3fn_x4
+ACT = mybir.ActivationFunctionType
+ALU = mybir.AluOpType
+AX = mybir.AxisListType
+
+P = 128
+B, T, D, O = 512, 32, 512, 128
+ROWS_PP = B * T // P
+SPP = ROWS_PP // T
+WORDS = D // 2
+UNIT = 4
+CHUNK = 8
+N_UNITS = ROWS_PP // UNIT
+FLOPS = 2 * B * T * D * O
+PAD_WORD = -(1.0 + 49024.0 / 8388608.0)
+
+
+def tile_linearnnencoder_t_kernel(tc, x, W, b, out):
+    nc = tc.nc
+    xv = x.flatten_outer_dims().rearrange("(p r) k -> p r k", p=P)
+    with tc.tile_pool(name="keep", bufs=1) as keep, tc.tile_pool(name="work", bufs=4) as work, tc.tile_pool(
+        name="ys", bufs=5
+    ) as ys, tc.psum_pool(name="pacc", bufs=1) as pacc, tc.psum_pool(name="pxt", bufs=4) as pxt, tc.psum_pool(
+        name="pmx", bufs=2
+    ) as pmx:
+        xs = []
+        for c in range(ROWS_PP // CHUNK):
+            xc = keep.tile([P, CHUNK, D], BF16, name="x%d" % c)
+            xs.append(xc)
+        nc.sync.dma_start(out=xs[0][:], in_=xv[:, 0:CHUNK, :])
+        w_sb = keep.tile([P, D], BF16)
+        nc.sync.dma_start(out=w_sb[:], in_=W)
+        bb = keep.tile([P, O], BF16)
+        nc.sync.dma_start(out=bb[:], in_=b.partition_broadcast(P))
+        for c in range(1, ROWS_PP // CHUNK):
+            nc.sync.dma_start(out=xs[c][:], in_=xv[:, c * CHUNK : (c + 1) * CHUNK, :])
+
+        ident = keep.tile([P, P], F32)
+        make_identity(nc, ident[:])
+        negc = keep.tile([P, 1], F32)
+        nc.vector.memset(negc[:], -PAD_WORD)
+
+        w_w = w_sb[:].bitcast(F32)
+        wt = pxt.tile([P, 2, 2, P], F32, tag="xt")
+        for u in range(2):
+            nc.tensor.transpose(wt[:, 0, u, :], w_w[:, u * P : (u + 1) * P], ident[:])
+        gw = keep.tile([P, O, 4], BF16, align_bytes=64)
+        nc.vector.tensor_copy(out=gw[:].bitcast(F32), in_=wt[:, 0, :, :].rearrange("q u o -> q o u"))
+        wc = keep.tile([P, O], U32, align_bytes=64)
+        wsc = keep.tile([P, O], U8, align_bytes=64)
+        nc.vector.quantize_mx(out=wc[:].bitcast(FP8X4), scales=wsc[:], in_=gw[:].rearrange("q o j -> q (o j)"))
+
+        bf = keep.tile([P, O], F32)
+        nc.vector.tensor_copy(out=bf[:], in_=bb[:])
+        bt = pxt.tile([P, 2, 2, P], F32, tag="xt")
+        nc.tensor.transpose(bt[:, 0, 0, :], bf[:], ident[:])
+        bcol = keep.tile([P, 1], F32)
+        nc.vector.tensor_copy(out=bcol[:], in_=bt[:, 0, 0, 0:1])
+        c0 = keep.tile([P, O], F32)
+        nc.scalar.activation(out=c0[:], in_=bf[:], func=ACT.Gelu)
+        c0sq = keep.tile([P, O], F32)
+        nc.vector.tensor_tensor(out=c0sq[:], in0=c0[:], in1=c0[:], op=ALU.mult)
+
+        dev = keep.tile([P, ROWS_PP], F32)
+        vf = keep.tile([P, ROWS_PP], F32)
+        sm = keep.tile([P, SPP, 8], F32)
+        res = keep.tile([P, SPP, 2 * O], F32)
+        acc_y = pacc.tile([P, SPP, O], F32)
+        acc_q = pacc.tile([P, SPP, O], F32)
+
+        for h in range(N_UNITS):
+            i0 = h * UNIT
+            xw = xs[i0 // CHUNK][:].bitcast(F32)
+            l0 = i0 % CHUNK
+            for a in range(UNIT):
+                junk = work.tile([P, WORDS], BF16, tag="junk")
+                nc.scalar.activation(
+                    out=junk[:],
+                    in_=xw[:, l0 + a, :],
+                    func=ACT.Square,
+                    bias=negc[:],
+                    scale=1.0,
+                    accum_out=dev[:, i0 + a : i0 + a + 1],
+                )
+            nc.vector.tensor_scalar(
+                out=vf[:, i0 : i0 + UNIT], in0=dev[:, i0 : i0 + UNIT], scalar1=0.0, scalar2=None, op0=ALU.not_equal
+            )
+            dg = work.tile([P, UNIT, P], F32, tag="dg")
+            for a in range(UNIT):
+                nc.vector.tensor_scalar(
+                    out=dg[:, a, :], in0=ident[:], scalar1=vf[:, i0 + a : i0 + a + 1], scalar2=None, op0=ALU.mult
+                )
+            g = work.tile([P, UNIT * P, 4], BF16, tag="g", align_bytes=64)
+            g_w = g[:].bitcast(F32)
+            for pr in range(UNIT // 2):
+                xt = pxt.tile([P, 2, 2, P], F32, tag="xt")
+                for a in range(2):
+                    for u in range(2):
+                        nc.tensor.transpose(
+                            xt[:, a, u, :], xw[:, l0 + 2 * pr + a, u * P : (u + 1) * P], dg[:, 2 * pr + a, :]
+                        )
+                dst = g_w[:, 2 * pr * P : (2 * pr + 2) * P, :].rearrange("q (a t) u -> q a t u", a=2)
+                src = xt[:].rearrange("q a u t -> q a t u")
+                if pr == 1 and h % 5 == 0:
+                    nc.scalar.copy(out=dst, in_=src)
+                else:
+                    nc.vector.tensor_copy(out=dst, in_=src)
+            codes = work.tile([P, UNIT * P], U32, tag="codes", align_bytes=64)
+            sc = work.tile([P, UNIT * P], U8, tag="sc", align_bytes=64)
+            nc.vector.quantize_mx(out=codes[:].bitcast(FP8X4), scales=sc[:], in_=g[:].rearrange("q t j -> q (t j)"))
+            v = pmx.tile([P, UNIT * P], F32, tag="v")
+            nc.tensor.matmul_mx(
+                out=v[:],
+                lhsT=wc[:].bitcast(FP8X4),
+                lhsT_scale=wsc[:],
+                rhs=codes[:].bitcast(FP8X4),
+                rhs_scale=sc[:],
+                start=True,
+                stop=True,
+            )
+            y = ys.tile([P, UNIT * P], F32, tag="y")
+            nc.scalar.activation(out=y[:], in_=v[:], func=ACT.Gelu, bias=bcol[:], scale=1.0)
+            q = ys.tile([P, UNIT * P], F32, tag="q")
+            nc.gpsimd.tensor_tensor(out=q[:], in0=y[:], in1=y[:], op=ALU.mult)
+            for a in range(UNIT):
+                j, t = (i0 + a) // T, (i0 + a) % T
+                nc.tensor.matmul(
+                    out=acc_y[:, j, :],
+                    lhsT=y[:, a * P : (a + 1) * P],
+                    rhs=ident[:],
+                    is_transpose=True,
+                    start=(t == 0),
+                    stop=(t == T - 1),
+                )
+                nc.tensor.matmul(
+                    out=acc_q[:, j, :],
+                    lhsT=q[:, a * P : (a + 1) * P],
+                    rhs=ident[:],
+                    is_transpose=True,
+                    start=(t == 0),
+                    stop=(t == T - 1),
+                )
+            if (i0 + UNIT) % T == 0:
+                j = i0 // T
+                n = sm[:, j, 0:1]
+                nc.vector.tensor_reduce(out=n, in_=vf[:, j * T : (j + 1) * T], axis=AX.X, op=ALU.add)
+                nc.vector.tensor_scalar(out=sm[:, j, 1:2], in0=n, scalar1=-float(T), scalar2=None, op0=ALU.add)
+                nc.vector.tensor_scalar(out=sm[:, j, 2:3], in0=n, scalar1=1.0, scalar2=None, op0=ALU.max)
+                nc.vector.tensor_scalar(out=sm[:, j, 3:4], in0=n, scalar1=-1.0, scalar2=1.0, op0=ALU.add, op1=ALU.max)
+                nc.vector.reciprocal(out=sm[:, j, 4:6], in_=sm[:, j, 2:4])
+                nc.vector.scalar_tensor_tensor(
+                    out=sm[:, j, 6:7], in0=n, scalar=0.0, in1=sm[:, j, 4:5], op0=ALU.is_gt, op1=ALU.mult
+                )
+                nc.vector.scalar_tensor_tensor(
+                    out=sm[:, j, 7:8], in0=n, scalar=1.0, in1=sm[:, j, 5:6], op0=ALU.is_gt, op1=ALU.mult
+                )
+                s1 = work.tile([P, O], F32, tag="s1")
+                nc.vector.scalar_tensor_tensor(
+                    out=s1[:], in0=c0[:], scalar=sm[:, j, 1:2], in1=acc_y[:, j, :], op0=ALU.mult, op1=ALU.add
+                )
+                s2 = work.tile([P, O], F32, tag="s2")
+                nc.vector.scalar_tensor_tensor(
+                    out=s2[:], in0=c0sq[:], scalar=sm[:, j, 1:2], in1=acc_q[:, j, :], op0=ALU.mult, op1=ALU.add
+                )
+                nc.vector.tensor_scalar(
+                    out=res[:, j, O : 2 * O], in0=s1[:], scalar1=sm[:, j, 6:7], scalar2=None, op0=ALU.mult
+                )
+                tt = work.tile([P, O], F32, tag="tt")
+                nc.vector.scalar_tensor_tensor(
+                    out=tt[:], in0=s1[:], scalar=sm[:, j, 6:7], in1=s1[:], op0=ALU.mult, op1=ALU.mult
+                )
+                nc.vector.tensor_tensor(out=s2[:], in0=s2[:], in1=tt[:], op=ALU.subtract)
+                nc.vector.tensor_scalar(
+                    out=res[:, j, 0:O], in0=s2[:], scalar1=sm[:, j, 7:8], scalar2=1e-30, op0=ALU.mult, op1=ALU.max
+                )
+        nc.scalar.activation(out=res[:, :, 0:O], in_=res[:, :, 0:O], func=ACT.Sqrt)
+        nc.sync.dma_start(out=out.rearrange("(p j) c -> p j c", j=SPP), in_=res[:])

@@ -1,3 +1,5 @@
+from contextlib import ExitStack
+
 import concourse.mybir as mybir
 from concourse.masks import make_identity
 
@@ -16,36 +18,63 @@ ROWS_PP = B * T // P
 SPP = ROWS_PP // T
 WORDS = D // 2
 UNIT = 4
-CHUNK = 8
-N_UNITS = ROWS_PP // UNIT
+NU = ROWS_PP // UNIT
+UPS = T // UNIT
 FLOPS = 2 * B * T * D * O
 PAD_WORD = -(1.0 + 49024.0 / 8388608.0)
+CHUNKS = [4, 4, 4, 4] + [8] * 14
+
+LA_TEST, LA_DIAG, LAG_Y, LAG_Q = 4, 2, 2, 3
+TAIL_S = 4
+PER_S = 5
+
+
+def evac_on_scalar(h, pr):
+    if pr == 0:
+        return False
+    return h >= NU - TAIL_S or h % PER_S == PER_S - 1
 
 
 def tile_linearnnencoder_t_kernel(tc, x, W, b, out):
     nc = tc.nc
     xv = x.flatten_outer_dims().rearrange("(p r) k -> p r k", p=P)
-    with tc.tile_pool(name="keep", bufs=1) as keep, tc.tile_pool(name="work", bufs=4) as work, tc.tile_pool(
-        name="ys", bufs=5
-    ) as ys, tc.psum_pool(name="pacc", bufs=1) as pacc, tc.psum_pool(name="pxt", bufs=4) as pxt, tc.psum_pool(
-        name="pmx", bufs=2
-    ) as pmx:
-        xs = []
-        for c in range(ROWS_PP // CHUNK):
-            xc = keep.tile([P, CHUNK, D], BF16, name="x%d" % c)
-            xs.append(xc)
-        nc.sync.dma_start(out=xs[0][:], in_=xv[:, 0:CHUNK, :])
+    ov = out.rearrange("(p j) c -> p j c", j=SPP)
+    with ExitStack() as ctx:
+        keep = ctx.enter_context(tc.tile_pool(name="keep", bufs=1))
+        jk = ctx.enter_context(tc.tile_pool(name="jk", bufs=2))
+        dgp = ctx.enter_context(tc.tile_pool(name="dgp", bufs=4))
+        gp = ctx.enter_context(tc.tile_pool(name="gp", bufs=3))
+        cp = ctx.enter_context(tc.tile_pool(name="cp", bufs=3))
+        ys = ctx.enter_context(tc.tile_pool(name="ys", bufs=6))
+        fin = ctx.enter_context(tc.tile_pool(name="fin", bufs=2))
+        pacc = ctx.enter_context(tc.psum_pool(name="pacc", bufs=1))
+        pxt = ctx.enter_context(tc.psum_pool(name="pxt", bufs=4))
+        pmx = ctx.enter_context(tc.psum_pool(name="pmx", bufs=2))
+        ctx.enter_context(tc.manual_schedule())
+
         w_sb = keep.tile([P, D], BF16)
         nc.sync.dma_start(out=w_sb[:], in_=W)
-        bb = keep.tile([P, O], BF16)
-        nc.sync.dma_start(out=bb[:], in_=b.partition_broadcast(P))
-        for c in range(1, ROWS_PP // CHUNK):
-            nc.sync.dma_start(out=xs[c][:], in_=xv[:, c * CHUNK : (c + 1) * CHUNK, :])
+        zb = keep.tile([P, O], BF16)
+        nc.vector.memset(zb[:], 0.0)
+        where = {}
+        r0 = 0
+        for c, n_t in enumerate(CHUNKS):
+            xc = keep.tile([P, n_t, D], BF16, name="x%d" % c)
+            nc.sync.dma_start(out=xc[:], in_=xv[:, r0 : r0 + n_t, :])
+            for k in range(n_t):
+                where[r0 + k] = (xc, k)
+            r0 += n_t
+            if c == 0:
+                nc.sync.dma_start(out=zb[0:1, :], in_=b.rearrange("(u o) -> u o", u=1))
 
         ident = keep.tile([P, P], F32)
         make_identity(nc, ident[:])
         negc = keep.tile([P, 1], F32)
         nc.vector.memset(negc[:], -PAD_WORD)
+        ones = keep.tile([P, P], BF16)
+        nc.vector.memset(ones[:], 1.0)
+        warm = keep.tile([P, 1], F32)
+        nc.scalar.activation(out=warm[:], in_=negc[:], func=ACT.Gelu)
 
         w_w = w_sb[:].bitcast(F32)
         wt = pxt.tile([P, 2, 2, P], F32, tag="xt")
@@ -57,128 +86,182 @@ def tile_linearnnencoder_t_kernel(tc, x, W, b, out):
         wsc = keep.tile([P, O], U8, align_bytes=64)
         nc.vector.quantize_mx(out=wc[:].bitcast(FP8X4), scales=wsc[:], in_=gw[:].rearrange("q o j -> q (o j)"))
 
-        bf = keep.tile([P, O], F32)
-        nc.vector.tensor_copy(out=bf[:], in_=bb[:])
         bt = pxt.tile([P, 2, 2, P], F32, tag="xt")
-        nc.tensor.transpose(bt[:, 0, 0, :], bf[:], ident[:])
+        nc.tensor.matmul(out=bt[:, 0, 0, :], lhsT=ones[:], rhs=zb[:], start=True, stop=True)
+        nc.tensor.matmul(out=bt[:, 1, 0, 0:64], lhsT=zb[:], rhs=ones[:, 0:64], start=True, stop=True)
         bcol = keep.tile([P, 1], F32)
-        nc.vector.tensor_copy(out=bcol[:], in_=bt[:, 0, 0, 0:1])
+        nc.vector.tensor_copy(out=bcol[:], in_=bt[:, 1, 0, 0:1])
         c0 = keep.tile([P, O], F32)
-        nc.scalar.activation(out=c0[:], in_=bf[:], func=ACT.Gelu)
         c0sq = keep.tile([P, O], F32)
-        nc.vector.tensor_tensor(out=c0sq[:], in0=c0[:], in1=c0[:], op=ALU.mult)
 
-        dev = keep.tile([P, ROWS_PP], F32)
-        vf = keep.tile([P, ROWS_PP], F32)
+        dev = keep.tile([P, NU, 8], F32)
+        vf = keep.tile([P, SPP, T], F32)
         sm = keep.tile([P, SPP, 8], F32)
         res = keep.tile([P, SPP, 2 * O], F32)
         acc_y = pacc.tile([P, SPP, O], F32)
         acc_q = pacc.tile([P, SPP, O], F32)
+        dg, xt, g, codes, sc, v, y, q = {}, {}, {}, {}, {}, {}, {}, {}
+        pre1, pre2 = {}, {}
 
-        for h in range(N_UNITS):
-            i0 = h * UNIT
-            xw = xs[i0 // CHUNK][:].bitcast(F32)
-            l0 = i0 % CHUNK
+        def row_words(i):
+            xc, k = where[i]
+            return xc[:].bitcast(F32)[:, k, :]
+
+        def test(h):
             for a in range(UNIT):
-                junk = work.tile([P, WORDS], BF16, tag="junk")
+                junk = jk.tile([P, WORDS], BF16, tag="junk")
                 nc.scalar.activation(
                     out=junk[:],
-                    in_=xw[:, l0 + a, :],
+                    in_=row_words(h * UNIT + a),
                     func=ACT.Square,
                     bias=negc[:],
                     scale=1.0,
-                    accum_out=dev[:, i0 + a : i0 + a + 1],
+                    accum_out=dev[:, h, a : a + 1],
                 )
-            nc.vector.tensor_scalar(
-                out=vf[:, i0 : i0 + UNIT], in0=dev[:, i0 : i0 + UNIT], scalar1=0.0, scalar2=None, op0=ALU.not_equal
-            )
-            dg = work.tile([P, UNIT, P], F32, tag="dg")
+
+        def diag(h):
+            dg[h] = dgp.tile([P, UNIT, P], F32, name="dg")
             for a in range(UNIT):
                 nc.vector.tensor_scalar(
-                    out=dg[:, a, :], in0=ident[:], scalar1=vf[:, i0 + a : i0 + a + 1], scalar2=None, op0=ALU.mult
+                    out=dg[h][:, a, :],
+                    in0=ident[:],
+                    scalar1=dev[:, h, a : a + 1],
+                    scalar2=0.0,
+                    op0=ALU.mult,
+                    op1=ALU.is_gt,
                 )
-            g = work.tile([P, UNIT * P, 4], BF16, tag="g", align_bytes=64)
-            g_w = g[:].bitcast(F32)
-            for pr in range(UNIT // 2):
-                xt = pxt.tile([P, 2, 2, P], F32, tag="xt")
+
+        def xpose(h):
+            for pr in range(2):
+                xt[h, pr] = pxt.tile([P, 2, 2, P], F32, name="xt")
                 for a in range(2):
+                    rw = row_words(h * UNIT + 2 * pr + a)
                     for u in range(2):
-                        nc.tensor.transpose(
-                            xt[:, a, u, :], xw[:, l0 + 2 * pr + a, u * P : (u + 1) * P], dg[:, 2 * pr + a, :]
-                        )
+                        nc.tensor.transpose(xt[h, pr][:, a, u, :], rw[:, u * P : (u + 1) * P], dg[h][:, 2 * pr + a, :])
+
+        def evac(h):
+            g[h] = gp.tile([P, UNIT * P, 4], BF16, name="g", align_bytes=64)
+            g_w = g[h][:].bitcast(F32)
+            for pr in range(2):
                 dst = g_w[:, 2 * pr * P : (2 * pr + 2) * P, :].rearrange("q (a t) u -> q a t u", a=2)
-                src = xt[:].rearrange("q a u t -> q a t u")
-                if pr == 1 and h % 5 == 0:
+                src = xt[h, pr][:].rearrange("q a u t -> q a t u")
+                if evac_on_scalar(h, pr):
                     nc.scalar.copy(out=dst, in_=src)
                 else:
                     nc.vector.tensor_copy(out=dst, in_=src)
-            codes = work.tile([P, UNIT * P], U32, tag="codes", align_bytes=64)
-            sc = work.tile([P, UNIT * P], U8, tag="sc", align_bytes=64)
-            nc.vector.quantize_mx(out=codes[:].bitcast(FP8X4), scales=sc[:], in_=g[:].rearrange("q t j -> q (t j)"))
-            v = pmx.tile([P, UNIT * P], F32, tag="v")
+
+        def quant(h):
+            codes[h] = cp.tile([P, UNIT * P], U32, name="codes", align_bytes=64)
+            sc[h] = cp.tile([P, UNIT * P], U8, name="sc", align_bytes=64)
+            nc.vector.quantize_mx(
+                out=codes[h][:].bitcast(FP8X4), scales=sc[h][:], in_=g[h][:].rearrange("q t j -> q (t j)")
+            )
+
+        def mx(h):
+            v[h] = pmx.tile([P, UNIT * P], F32, name="v")
             nc.tensor.matmul_mx(
-                out=v[:],
+                out=v[h][:],
                 lhsT=wc[:].bitcast(FP8X4),
                 lhsT_scale=wsc[:],
-                rhs=codes[:].bitcast(FP8X4),
-                rhs_scale=sc[:],
+                rhs=codes[h][:].bitcast(FP8X4),
+                rhs_scale=sc[h][:],
                 start=True,
                 stop=True,
             )
-            y = ys.tile([P, UNIT * P], F32, tag="y")
-            nc.scalar.activation(out=y[:], in_=v[:], func=ACT.Gelu, bias=bcol[:], scale=1.0)
-            q = ys.tile([P, UNIT * P], F32, tag="q")
-            nc.gpsimd.tensor_tensor(out=q[:], in0=y[:], in1=y[:], op=ALU.mult)
+
+        def gelu(h):
+            y[h] = ys.tile([P, UNIT * P], F32, name="y")
+            nc.scalar.activation(out=y[h][:], in_=v[h][:], func=ACT.Gelu, bias=bcol[:], scale=1.0)
+
+        def square(h):
+            q[h] = ys.tile([P, UNIT * P], F32, name="q")
+            if h == NU - 1:
+                nc.scalar.activation(out=q[h][:], in_=y[h][:], func=ACT.Square)
+            else:
+                nc.gpsimd.tensor_tensor(out=q[h][:], in0=y[h][:], in1=y[h][:], op=ALU.mult)
+
+        def accumulate(h, src, acc):
             for a in range(UNIT):
-                j, t = (i0 + a) // T, (i0 + a) % T
+                j, t = (h * UNIT + a) // T, (h * UNIT + a) % T
                 nc.tensor.matmul(
-                    out=acc_y[:, j, :],
-                    lhsT=y[:, a * P : (a + 1) * P],
+                    out=acc[:, j, :],
+                    lhsT=src[h][:, a * P : (a + 1) * P],
                     rhs=ident[:],
                     is_transpose=True,
                     start=(t == 0),
                     stop=(t == T - 1),
                 )
-                nc.tensor.matmul(
-                    out=acc_q[:, j, :],
-                    lhsT=q[:, a * P : (a + 1) * P],
-                    rhs=ident[:],
-                    is_transpose=True,
-                    start=(t == 0),
-                    stop=(t == T - 1),
-                )
-            if (i0 + UNIT) % T == 0:
-                j = i0 // T
-                n = sm[:, j, 0:1]
-                nc.vector.tensor_reduce(out=n, in_=vf[:, j * T : (j + 1) * T], axis=AX.X, op=ALU.add)
-                nc.vector.tensor_scalar(out=sm[:, j, 1:2], in0=n, scalar1=-float(T), scalar2=None, op0=ALU.add)
-                nc.vector.tensor_scalar(out=sm[:, j, 2:3], in0=n, scalar1=1.0, scalar2=None, op0=ALU.max)
-                nc.vector.tensor_scalar(out=sm[:, j, 3:4], in0=n, scalar1=-1.0, scalar2=1.0, op0=ALU.add, op1=ALU.max)
-                nc.vector.reciprocal(out=sm[:, j, 4:6], in_=sm[:, j, 2:4])
-                nc.vector.scalar_tensor_tensor(
-                    out=sm[:, j, 6:7], in0=n, scalar=0.0, in1=sm[:, j, 4:5], op0=ALU.is_gt, op1=ALU.mult
-                )
-                nc.vector.scalar_tensor_tensor(
-                    out=sm[:, j, 7:8], in0=n, scalar=1.0, in1=sm[:, j, 5:6], op0=ALU.is_gt, op1=ALU.mult
-                )
-                s1 = work.tile([P, O], F32, tag="s1")
-                nc.vector.scalar_tensor_tensor(
-                    out=s1[:], in0=c0[:], scalar=sm[:, j, 1:2], in1=acc_y[:, j, :], op0=ALU.mult, op1=ALU.add
-                )
-                s2 = work.tile([P, O], F32, tag="s2")
-                nc.vector.scalar_tensor_tensor(
-                    out=s2[:], in0=c0sq[:], scalar=sm[:, j, 1:2], in1=acc_q[:, j, :], op0=ALU.mult, op1=ALU.add
-                )
-                nc.vector.tensor_scalar(
-                    out=res[:, j, O : 2 * O], in0=s1[:], scalar1=sm[:, j, 6:7], scalar2=None, op0=ALU.mult
-                )
-                tt = work.tile([P, O], F32, tag="tt")
-                nc.vector.scalar_tensor_tensor(
-                    out=tt[:], in0=s1[:], scalar=sm[:, j, 6:7], in1=s1[:], op0=ALU.mult, op1=ALU.mult
-                )
-                nc.vector.tensor_tensor(out=s2[:], in0=s2[:], in1=tt[:], op=ALU.subtract)
-                nc.vector.tensor_scalar(
-                    out=res[:, j, 0:O], in0=s2[:], scalar1=sm[:, j, 7:8], scalar2=1e-30, op0=ALU.mult, op1=ALU.max
-                )
-        nc.scalar.activation(out=res[:, :, 0:O], in_=res[:, :, 0:O], func=ACT.Sqrt)
-        nc.sync.dma_start(out=out.rearrange("(p j) c -> p j c", j=SPP), in_=res[:])
+
+        def counts(j):
+            nc.vector.tensor_scalar(
+                out=vf[:, j, :].rearrange("p (h a) -> p h a", a=UNIT),
+                in0=dev[:, j * UPS : (j + 1) * UPS, 0:UNIT],
+                scalar1=0.0,
+                scalar2=None,
+                op0=ALU.is_gt,
+            )
+            n = sm[:, j, 0:1]
+            nc.vector.tensor_reduce(out=n, in_=vf[:, j, :], axis=AX.X, op=ALU.add)
+            nc.vector.tensor_scalar(out=sm[:, j, 1:2], in0=n, scalar1=-float(T), scalar2=None, op0=ALU.add)
+            nc.vector.tensor_scalar(out=sm[:, j, 2:3], in0=n, scalar1=1.0, scalar2=None, op0=ALU.max)
+            nc.vector.tensor_scalar(out=sm[:, j, 3:4], in0=n, scalar1=-1.0, scalar2=1.0, op0=ALU.add, op1=ALU.max)
+            nc.vector.reciprocal(out=sm[:, j, 4:6], in_=sm[:, j, 2:4])
+            nc.vector.scalar_tensor_tensor(
+                out=sm[:, j, 6:7], in0=n, scalar=0.0, in1=sm[:, j, 4:5], op0=ALU.is_gt, op1=ALU.mult
+            )
+            nc.vector.scalar_tensor_tensor(
+                out=sm[:, j, 7:8], in0=n, scalar=1.0, in1=sm[:, j, 5:6], op0=ALU.is_gt, op1=ALU.mult
+            )
+            pre1[j] = fin.tile([P, O], F32, name="pre1")
+            nc.vector.tensor_scalar(out=pre1[j][:], in0=c0[:], scalar1=sm[:, j, 1:2], scalar2=None, op0=ALU.mult)
+            pre2[j] = fin.tile([P, O], F32, name="pre2")
+            nc.vector.tensor_scalar(out=pre2[j][:], in0=c0sq[:], scalar1=sm[:, j, 1:2], scalar2=None, op0=ALU.mult)
+
+        def finish_mean(j):
+            s1 = fin.tile([P, O], F32, name="s1")
+            nc.vector.tensor_tensor(out=s1[:], in0=pre1[j][:], in1=acc_y[:, j, :], op=ALU.add)
+            nc.vector.tensor_scalar(
+                out=res[:, j, O : 2 * O], in0=s1[:], scalar1=sm[:, j, 6:7], scalar2=None, op0=ALU.mult
+            )
+            tt = fin.tile([P, O], F32, name="tt")
+            nc.vector.tensor_tensor(out=tt[:], in0=res[:, j, O : 2 * O], in1=s1[:], op=ALU.mult)
+            nc.vector.tensor_tensor(out=pre2[j][:], in0=pre2[j][:], in1=tt[:], op=ALU.subtract)
+
+        def finish_var(j):
+            d = fin.tile([P, O], F32, name="d")
+            nc.vector.tensor_tensor(out=d[:], in0=pre2[j][:], in1=acc_q[:, j, :], op=ALU.add)
+            nc.vector.tensor_scalar(
+                out=res[:, j, 0:O], in0=d[:], scalar1=sm[:, j, 7:8], scalar2=1e-30, op0=ALU.mult, op1=ALU.max
+            )
+
+        def on(stage, h):
+            if 0 <= h < NU:
+                stage(h)
+
+        for s in range(-LA_TEST, NU + LAG_Q + 3):
+            on(evac, s)
+            on(gelu, s - 2)
+            on(quant, s - 1)
+            on(test, s + LA_TEST)
+            if s == -LA_TEST:
+                nc.scalar.activation(out=c0[:], in_=bt[:, 0, 0, :], func=ACT.Gelu)
+                nc.scalar.activation(out=c0sq[:], in_=c0[:], func=ACT.Square)
+            on(diag, s + LA_DIAG)
+            on(xpose, s + LA_DIAG)
+            on(mx, s - 1)
+            on(square, s - 2)
+            on(lambda h: accumulate(h, y, acc_y), s - LAG_Y)
+            on(lambda h: accumulate(h, q, acc_q), s - LAG_Q)
+            last = s + LA_DIAG
+            if 0 <= last < NU and last % UPS == UPS - 1:
+                counts(last // UPS)
+            for j in range(SPP):
+                lag = 2 if j < SPP - 1 else 0
+                if s - LAG_Y - lag == j * UPS + UPS - 1:
+                    finish_mean(j)
+                if s - LAG_Q - lag == j * UPS + UPS - 1:
+                    finish_var(j)
+        nc.scalar.activation(out=res[:, 0 : SPP - 1, 0:O], in_=res[:, 0 : SPP - 1, 0:O], func=ACT.Sqrt)
+        nc.sync.dma_start(out=ov[:, 0 : SPP - 1, :], in_=res[:, 0 : SPP - 1, :])
+        nc.scalar.activation(out=res[:, SPP - 1, 0:O], in_=res[:, SPP - 1, 0:O], func=ACT.Sqrt)
+        nc.sync.dma_start(out=ov[:, SPP - 1, :], in_=res[:, SPP - 1, :])

@@ -25,8 +25,9 @@ PAD_WORD = -(1.0 + 49024.0 / 8388608.0)
 CHUNKS = [4, 4, 4, 4] + [8] * 14
 
 LA_TEST, LA_DIAG, LAG_Y, LAG_Q = 4, 2, 2, 3
-TAIL_S = 4
-PER_S = 5
+TAIL_S = 3
+PER_S = 6
+N_IDLE = 1
 
 
 def evac_on_scalar(h, pr):
@@ -85,6 +86,36 @@ def tile_linearnnencoder_t_kernel(tc, x, W, b, out):
         wc = keep.tile([P, O], U32, align_bytes=64)
         wsc = keep.tile([P, O], U8, align_bytes=64)
         nc.vector.quantize_mx(out=wc[:].bitcast(FP8X4), scales=wsc[:], in_=gw[:].rearrange("q o j -> q (o j)"))
+
+        def idle_pass(dst, h):
+            if h >= 0:
+                nc.tensor.matmul_mx(
+                    out=dst[:],
+                    lhsT=wc[:].bitcast(FP8X4),
+                    lhsT_scale=wsc[:],
+                    rhs=codes[h][:].bitcast(FP8X4),
+                    rhs_scale=sc[h][:],
+                    start=True,
+                    stop=True,
+                )
+            else:
+                for k in range(UNIT):
+                    nc.tensor.matmul_mx(
+                        out=dst[:, k * P : (k + 1) * P],
+                        lhsT=wc[:].bitcast(FP8X4),
+                        lhsT_scale=wsc[:],
+                        rhs=wc[:].bitcast(FP8X4),
+                        rhs_scale=wsc[:],
+                        start=True,
+                        stop=True,
+                    )
+
+        def idle_run(n):
+            vd = pmx.tile([P, UNIT * P], F32, name="v")
+            for k in range(n):
+                idle_pass(vd, -1)
+
+        idle_run(3)
 
         bt = pxt.tile([P, 2, 2, P], F32, tag="xt")
         nc.tensor.matmul(out=bt[:, 0, 0, :], lhsT=ones[:], rhs=zb[:], start=True, stop=True)
@@ -159,6 +190,8 @@ def tile_linearnnencoder_t_kernel(tc, x, W, b, out):
 
         def mx(h):
             v[h] = pmx.tile([P, UNIT * P], F32, name="v")
+            for k in range(N_IDLE):
+                idle_pass(v[h], h - 1)
             nc.tensor.matmul_mx(
                 out=v[h][:],
                 lhsT=wc[:].bitcast(FP8X4),
@@ -248,6 +281,8 @@ def tile_linearnnencoder_t_kernel(tc, x, W, b, out):
                 nc.scalar.activation(out=c0sq[:], in_=c0[:], func=ACT.Square)
             on(diag, s + LA_DIAG)
             on(xpose, s + LA_DIAG)
+            if s < 1:
+                idle_run(2)
             on(mx, s - 1)
             on(square, s - 2)
             on(lambda h: accumulate(h, y, acc_y), s - LAG_Y)

@@ -27,7 +27,7 @@ CHUNKS = [4, 4, 4, 4] + [8] * 14
 LA_TEST, LA_DIAG, LAG_Y, LAG_Q = 4, 2, 2, 3
 TAIL_S = 3
 PER_S = 6
-N_IDLE = 1
+N_IDLE = 2
 
 
 def evac_on_scalar(h, pr):

@@ -24,16 +24,17 @@ FLOPS = 2 * B * T * D * O
 PAD_WORD = -(1.0 + 49024.0 / 8388608.0)
 CHUNKS = [4, 4, 4, 4] + [8] * 14
 
-LA_TEST, LA_DIAG, LAG_Y, LAG_Q = 4, 2, 2, 3
+LA_TEST, LA_DIAG, LAG_Y, LAG_Q = 4, 2, 2, 4
 TAIL_S = 3
-PER_S = 6
 N_IDLE = 2
 
 
 def evac_on_scalar(h, pr):
-    if pr == 0:
-        return False
-    return h >= NU - TAIL_S or h % PER_S == PER_S - 1
+    return pr == 1 and h >= NU - TAIL_S
+
+
+def square_on_vector(h):
+    return h % 3 == 2 and h < NU - 2
 
 
 def tile_linearnnencoder_t_kernel(tc, x, W, b, out):
@@ -208,10 +209,10 @@ def tile_linearnnencoder_t_kernel(tc, x, W, b, out):
 
         def square(h):
             q[h] = ys.tile([P, UNIT * P], F32, name="q")
-            if h == NU - 1:
-                nc.scalar.activation(out=q[h][:], in_=y[h][:], func=ACT.Square)
+            if square_on_vector(h):
+                nc.vector.tensor_tensor(out=q[h][:], in0=y[h][:], in1=y[h][:], op=ALU.mult)
             else:
-                nc.gpsimd.tensor_tensor(out=q[h][:], in0=y[h][:], in1=y[h][:], op=ALU.mult)
+                nc.scalar.activation(out=q[h][:], in_=y[h][:], func=ACT.Square)
 
         def accumulate(h, src, acc):
             for a in range(UNIT):
@@ -284,7 +285,10 @@ def tile_linearnnencoder_t_kernel(tc, x, W, b, out):
             if s < 1:
                 idle_run(2)
             on(mx, s - 1)
-            on(square, s - 2)
+            if not square_on_vector(s - 2):
+                on(square, s - 2)
+            if square_on_vector(s - 3):
+                on(square, s - 3)
             on(lambda h: accumulate(h, y, acc_y), s - LAG_Y)
             on(lambda h: accumulate(h, q, acc_q), s - LAG_Q)
             last = s + LA_DIAG

@@ -24,17 +24,13 @@ FLOPS = 2 * B * T * D * O
 PAD_WORD = -(1.0 + 49024.0 / 8388608.0)
 CHUNKS = [4, 4, 4, 4] + [8] * 14
 
-LA_TEST, LA_DIAG, LAG_Y, LAG_Q = 4, 2, 2, 4
+LA_TEST, LA_DIAG, LAG_FOLD, LAG_ACC = 4, 2, 3, 4
 TAIL_S = 3
-N_IDLE = 2
+PER_S = 4
 
 
 def evac_on_scalar(h, pr):
-    return pr == 1 and h >= NU - TAIL_S
-
-
-def square_on_vector(h):
-    return h % 3 == 2 and h < NU - 2
+    return pr == 1 and (h >= NU - TAIL_S or h % PER_S == PER_S - 1)
 
 
 def tile_linearnnencoder_t_kernel(tc, x, W, b, out):
@@ -47,7 +43,8 @@ def tile_linearnnencoder_t_kernel(tc, x, W, b, out):
         dgp = ctx.enter_context(tc.tile_pool(name="dgp", bufs=4))
         gp = ctx.enter_context(tc.tile_pool(name="gp", bufs=3))
         cp = ctx.enter_context(tc.tile_pool(name="cp", bufs=3))
-        ys = ctx.enter_context(tc.tile_pool(name="ys", bufs=6))
+        ys = ctx.enter_context(tc.tile_pool(name="ys", bufs=4))
+        fs = ctx.enter_context(tc.tile_pool(name="fs", bufs=3))
         fin = ctx.enter_context(tc.tile_pool(name="fin", bufs=2))
         pacc = ctx.enter_context(tc.psum_pool(name="pacc", bufs=1))
         pxt = ctx.enter_context(tc.psum_pool(name="pxt", bufs=4))
@@ -88,36 +85,6 @@ def tile_linearnnencoder_t_kernel(tc, x, W, b, out):
         wsc = keep.tile([P, O], U8, align_bytes=64)
         nc.vector.quantize_mx(out=wc[:].bitcast(FP8X4), scales=wsc[:], in_=gw[:].rearrange("q o j -> q (o j)"))
 
-        def idle_pass(dst, h):
-            if h >= 0:
-                nc.tensor.matmul_mx(
-                    out=dst[:],
-                    lhsT=wc[:].bitcast(FP8X4),
-                    lhsT_scale=wsc[:],
-                    rhs=codes[h][:].bitcast(FP8X4),
-                    rhs_scale=sc[h][:],
-                    start=True,
-                    stop=True,
-                )
-            else:
-                for k in range(UNIT):
-                    nc.tensor.matmul_mx(
-                        out=dst[:, k * P : (k + 1) * P],
-                        lhsT=wc[:].bitcast(FP8X4),
-                        lhsT_scale=wsc[:],
-                        rhs=wc[:].bitcast(FP8X4),
-                        rhs_scale=wsc[:],
-                        start=True,
-                        stop=True,
-                    )
-
-        def idle_run(n):
-            vd = pmx.tile([P, UNIT * P], F32, name="v")
-            for k in range(n):
-                idle_pass(vd, -1)
-
-        idle_run(3)
-
         bt = pxt.tile([P, 2, 2, P], F32, tag="xt")
         nc.tensor.matmul(out=bt[:, 0, 0, :], lhsT=ones[:], rhs=zb[:], start=True, stop=True)
         nc.tensor.matmul(out=bt[:, 1, 0, 0:64], lhsT=zb[:], rhs=ones[:, 0:64], start=True, stop=True)
@@ -132,7 +99,7 @@ def tile_linearnnencoder_t_kernel(tc, x, W, b, out):
         res = keep.tile([P, SPP, 2 * O], F32)
         acc_y = pacc.tile([P, SPP, O], F32)
         acc_q = pacc.tile([P, SPP, O], F32)
-        dg, xt, g, codes, sc, v, y, q = {}, {}, {}, {}, {}, {}, {}, {}
+        dg, xt, g, codes, sc, v, y, q, yf, qf = {}, {}, {}, {}, {}, {}, {}, {}, {}, {}
         pre1, pre2 = {}, {}
 
         def row_words(i):
@@ -191,8 +158,6 @@ def tile_linearnnencoder_t_kernel(tc, x, W, b, out):
 
         def mx(h):
             v[h] = pmx.tile([P, UNIT * P], F32, name="v")
-            for k in range(N_IDLE):
-                idle_pass(v[h], h - 1)
             nc.tensor.matmul_mx(
                 out=v[h][:],
                 lhsT=wc[:].bitcast(FP8X4),
@@ -209,22 +174,29 @@ def tile_linearnnencoder_t_kernel(tc, x, W, b, out):
 
         def square(h):
             q[h] = ys.tile([P, UNIT * P], F32, name="q")
-            if square_on_vector(h):
-                nc.vector.tensor_tensor(out=q[h][:], in0=y[h][:], in1=y[h][:], op=ALU.mult)
-            else:
-                nc.scalar.activation(out=q[h][:], in_=y[h][:], func=ACT.Square)
+            nc.scalar.activation(out=q[h][:], in_=y[h][:], func=ACT.Square)
 
-        def accumulate(h, src, acc):
-            for a in range(UNIT):
-                j, t = (h * UNIT + a) // T, (h * UNIT + a) % T
-                nc.tensor.matmul(
-                    out=acc[:, j, :],
-                    lhsT=src[h][:, a * P : (a + 1) * P],
-                    rhs=ident[:],
-                    is_transpose=True,
-                    start=(t == 0),
-                    stop=(t == T - 1),
-                )
+        def fold(h):
+            half = UNIT * P // 2
+            yf[h] = fs.tile([P, half], F32, name="yf")
+            nc.vector.tensor_tensor(out=yf[h][:], in0=y[h][:, 0:half], in1=y[h][:, half : 2 * half], op=ALU.add)
+            qf[h] = fs.tile([P, half], F32, name="qf")
+            nc.vector.tensor_tensor(out=qf[h][:], in0=q[h][:, 0:half], in1=q[h][:, half : 2 * half], op=ALU.add)
+
+        def accumulate(h):
+            j = h // UPS
+            for a in range(UNIT // 2):
+                first = h % UPS == 0 and a == 0
+                final = h % UPS == UPS - 1 and a == UNIT // 2 - 1
+                for src, acc in ((yf, acc_y), (qf, acc_q)):
+                    nc.tensor.matmul(
+                        out=acc[:, j, :],
+                        lhsT=src[h][:, a * P : (a + 1) * P],
+                        rhs=ident[:],
+                        is_transpose=True,
+                        start=first,
+                        stop=final,
+                    )
 
         def counts(j):
             nc.vector.tensor_scalar(
@@ -272,7 +244,7 @@ def tile_linearnnencoder_t_kernel(tc, x, W, b, out):
             if 0 <= h < NU:
                 stage(h)
 
-        for s in range(-LA_TEST, NU + LAG_Q + 3):
+        for s in range(-LA_TEST, NU + LAG_ACC + 3):
             on(evac, s)
             on(gelu, s - 2)
             on(quant, s - 1)
@@ -282,23 +254,17 @@ def tile_linearnnencoder_t_kernel(tc, x, W, b, out):
                 nc.scalar.activation(out=c0sq[:], in_=c0[:], func=ACT.Square)
             on(diag, s + LA_DIAG)
             on(xpose, s + LA_DIAG)
-            if s < 1:
-                idle_run(2)
             on(mx, s - 1)
-            if not square_on_vector(s - 2):
-                on(square, s - 2)
-            if square_on_vector(s - 3):
-                on(square, s - 3)
-            on(lambda h: accumulate(h, y, acc_y), s - LAG_Y)
-            on(lambda h: accumulate(h, q, acc_q), s - LAG_Q)
+            on(square, s - 2)
+            on(fold, s - LAG_FOLD)
+            on(accumulate, s - LAG_ACC)
             last = s + LA_DIAG
             if 0 <= last < NU and last % UPS == UPS - 1:
                 counts(last // UPS)
             for j in range(SPP):
                 lag = 2 if j < SPP - 1 else 0
-                if s - LAG_Y - lag == j * UPS + UPS - 1:
+                if s - LAG_ACC - lag == j * UPS + UPS - 1:
                     finish_mean(j)
-                if s - LAG_Q - lag == j * UPS + UPS - 1:
                     finish_var(j)
         nc.scalar.activation(out=res[:, 0 : SPP - 1, 0:O], in_=res[:, 0 : SPP - 1, 0:O], func=ACT.Sqrt)
         nc.sync.dma_start(out=ov[:, 0 : SPP - 1, :], in_=res[:, 0 : SPP - 1, :])

@@ -24,13 +24,18 @@ FLOPS = 2 * B * T * D * O
 PAD_WORD = -(1.0 + 49024.0 / 8388608.0)
 CHUNKS = [4, 4, 4, 4] + [8] * 14
 
-LA_TEST, LA_DIAG, LAG_FOLD, LAG_ACC = 4, 2, 3, 4
+LA_TEST, LA_DIAG, LA_XPOSE = 5, 3, 2
+LAG_QUANT, LAG_GELU, LAG_SQ_V, LAG_ACC = 1, 3, 4, 5
 TAIL_S = 3
-PER_S = 4
+PER_SQ_V = 8
 
 
 def evac_on_scalar(h, pr):
-    return pr == 1 and (h >= NU - TAIL_S or h % PER_S == PER_S - 1)
+    return pr == 1 and h >= NU - TAIL_S
+
+
+def square_on_vector(h):
+    return h % PER_SQ_V == PER_SQ_V - 1 and h < NU - 2
 
 
 def tile_linearnnencoder_t_kernel(tc, x, W, b, out):
@@ -40,16 +45,15 @@ def tile_linearnnencoder_t_kernel(tc, x, W, b, out):
     with ExitStack() as ctx:
         keep = ctx.enter_context(tc.tile_pool(name="keep", bufs=1))
         jk = ctx.enter_context(tc.tile_pool(name="jk", bufs=2))
-        dgp = ctx.enter_context(tc.tile_pool(name="dgp", bufs=4))
-        gp = ctx.enter_context(tc.tile_pool(name="gp", bufs=3))
-        cp = ctx.enter_context(tc.tile_pool(name="cp", bufs=3))
-        ys = ctx.enter_context(tc.tile_pool(name="ys", bufs=4))
-        fs = ctx.enter_context(tc.tile_pool(name="fs", bufs=3))
+        dgp = ctx.enter_context(tc.tile_pool(name="dgp", bufs=5))
+        gp = ctx.enter_context(tc.tile_pool(name="gp", bufs=4))
+        cp = ctx.enter_context(tc.tile_pool(name="cp", bufs=4))
+        ys = ctx.enter_context(tc.tile_pool(name="ys", bufs=6))
+        fs = ctx.enter_context(tc.tile_pool(name="fs", bufs=4))
         fin = ctx.enter_context(tc.tile_pool(name="fin", bufs=2))
         pacc = ctx.enter_context(tc.psum_pool(name="pacc", bufs=1))
         pxt = ctx.enter_context(tc.psum_pool(name="pxt", bufs=4))
         pmx = ctx.enter_context(tc.psum_pool(name="pmx", bufs=2))
-        ctx.enter_context(tc.manual_schedule())
 
         w_sb = keep.tile([P, D], BF16)
         nc.sync.dma_start(out=w_sb[:], in_=W)
@@ -99,7 +103,7 @@ def tile_linearnnencoder_t_kernel(tc, x, W, b, out):
         res = keep.tile([P, SPP, 2 * O], F32)
         acc_y = pacc.tile([P, SPP, O], F32)
         acc_q = pacc.tile([P, SPP, O], F32)
-        dg, xt, g, codes, sc, v, y, q, yf, qf = {}, {}, {}, {}, {}, {}, {}, {}, {}, {}
+        dg, xt, g, codes, sc, v, y, q, yf = {}, {}, {}, {}, {}, {}, {}, {}, {}
         pre1, pre2 = {}, {}
 
         def row_words(i):
@@ -174,28 +178,27 @@ def tile_linearnnencoder_t_kernel(tc, x, W, b, out):
 
         def square(h):
             q[h] = ys.tile([P, UNIT * P], F32, name="q")
-            nc.scalar.activation(out=q[h][:], in_=y[h][:], func=ACT.Square)
+            if square_on_vector(h):
+                nc.vector.tensor_tensor(out=q[h][:], in0=y[h][:], in1=y[h][:], op=ALU.mult)
+            else:
+                nc.scalar.activation(out=q[h][:], in_=y[h][:], func=ACT.Square)
 
         def fold(h):
             half = UNIT * P // 2
             yf[h] = fs.tile([P, half], F32, name="yf")
             nc.vector.tensor_tensor(out=yf[h][:], in0=y[h][:, 0:half], in1=y[h][:, half : 2 * half], op=ALU.add)
-            qf[h] = fs.tile([P, half], F32, name="qf")
-            nc.vector.tensor_tensor(out=qf[h][:], in0=q[h][:, 0:half], in1=q[h][:, half : 2 * half], op=ALU.add)
 
         def accumulate(h):
             j = h // UPS
-            for a in range(UNIT // 2):
-                first = h % UPS == 0 and a == 0
-                final = h % UPS == UPS - 1 and a == UNIT // 2 - 1
-                for src, acc in ((yf, acc_y), (qf, acc_q)):
+            for src, acc, n_t in ((yf, acc_y, UNIT // 2), (q, acc_q, UNIT)):
+                for a in range(n_t):
                     nc.tensor.matmul(
                         out=acc[:, j, :],
                         lhsT=src[h][:, a * P : (a + 1) * P],
                         rhs=ident[:],
                         is_transpose=True,
-                        start=first,
-                        stop=final,
+                        start=(h % UPS == 0 and a == 0),
+                        stop=(h % UPS == UPS - 1 and a == n_t - 1),
                     )
 
         def counts(j):
@@ -246,17 +249,20 @@ def tile_linearnnencoder_t_kernel(tc, x, W, b, out):
 
         for s in range(-LA_TEST, NU + LAG_ACC + 3):
             on(evac, s)
-            on(gelu, s - 2)
-            on(quant, s - 1)
+            on(gelu, s - LAG_GELU)
+            if not square_on_vector(s - LAG_GELU):
+                on(square, s - LAG_GELU)
             on(test, s + LA_TEST)
             if s == -LA_TEST:
                 nc.scalar.activation(out=c0[:], in_=bt[:, 0, 0, :], func=ACT.Gelu)
                 nc.scalar.activation(out=c0sq[:], in_=c0[:], func=ACT.Square)
+            if square_on_vector(s - LAG_SQ_V):
+                on(square, s - LAG_SQ_V)
+            on(quant, s - LAG_QUANT)
             on(diag, s + LA_DIAG)
-            on(xpose, s + LA_DIAG)
-            on(mx, s - 1)
-            on(square, s - 2)
-            on(fold, s - LAG_FOLD)
+            on(fold, s - LAG_ACC)
+            on(xpose, s + LA_XPOSE)
+            on(mx, s - LAG_QUANT)
             on(accumulate, s - LAG_ACC)
             last = s + LA_DIAG
             if 0 <= last < NU and last % UPS == UPS - 1:

@@ -22,12 +22,12 @@ NU = ROWS_PP // UNIT
 UPS = T // UNIT
 FLOPS = 2 * B * T * D * O
 PAD_WORD = -(1.0 + 49024.0 / 8388608.0)
-CHUNKS = [4, 4, 4, 4] + [8] * 14
+CHUNKS = [2, 2, 4, 4, 4] + [8] * 14
 
 LA_TEST, LA_DIAG, LA_XPOSE = 5, 3, 2
 LAG_QUANT, LAG_GELU, LAG_SQ_V, LAG_ACC = 1, 3, 4, 5
 TAIL_S = 3
-PER_SQ_V = 8
+PER_SQ_V = 2
 
 
 def evac_on_scalar(h, pr):
@@ -49,14 +49,12 @@ def tile_linearnnencoder_t_kernel(tc, x, W, b, out):
         gp = ctx.enter_context(tc.tile_pool(name="gp", bufs=4))
         cp = ctx.enter_context(tc.tile_pool(name="cp", bufs=4))
         ys = ctx.enter_context(tc.tile_pool(name="ys", bufs=6))
-        fs = ctx.enter_context(tc.tile_pool(name="fs", bufs=4))
         fin = ctx.enter_context(tc.tile_pool(name="fin", bufs=2))
         pacc = ctx.enter_context(tc.psum_pool(name="pacc", bufs=1))
         pxt = ctx.enter_context(tc.psum_pool(name="pxt", bufs=4))
         pmx = ctx.enter_context(tc.psum_pool(name="pmx", bufs=2))
 
         w_sb = keep.tile([P, D], BF16)
-        nc.sync.dma_start(out=w_sb[:], in_=W)
         zb = keep.tile([P, O], BF16)
         nc.vector.memset(zb[:], 0.0)
         where = {}
@@ -68,6 +66,7 @@ def tile_linearnnencoder_t_kernel(tc, x, W, b, out):
                 where[r0 + k] = (xc, k)
             r0 += n_t
             if c == 0:
+                nc.sync.dma_start(out=w_sb[:], in_=W)
                 nc.sync.dma_start(out=zb[0:1, :], in_=b.rearrange("(u o) -> u o", u=1))
 
         ident = keep.tile([P, P], F32)
@@ -103,7 +102,7 @@ def tile_linearnnencoder_t_kernel(tc, x, W, b, out):
         res = keep.tile([P, SPP, 2 * O], F32)
         acc_y = pacc.tile([P, SPP, O], F32)
         acc_q = pacc.tile([P, SPP, O], F32)
-        dg, xt, g, codes, sc, v, y, q, yf = {}, {}, {}, {}, {}, {}, {}, {}, {}
+        dg, xt, g, codes, sc, v, y, q = {}, {}, {}, {}, {}, {}, {}, {}
         pre1, pre2 = {}, {}
 
         def row_words(i):
@@ -183,14 +182,9 @@ def tile_linearnnencoder_t_kernel(tc, x, W, b, out):
             else:
                 nc.scalar.activation(out=q[h][:], in_=y[h][:], func=ACT.Square)
 
-        def fold(h):
-            half = UNIT * P // 2
-            yf[h] = fs.tile([P, half], F32, name="yf")
-            nc.vector.tensor_tensor(out=yf[h][:], in0=y[h][:, 0:half], in1=y[h][:, half : 2 * half], op=ALU.add)
-
         def accumulate(h):
             j = h // UPS
-            for src, acc, n_t in ((yf, acc_y, UNIT // 2), (q, acc_q, UNIT)):
+            for src, acc, n_t in ((y, acc_y, UNIT), (q, acc_q, UNIT)):
                 for a in range(n_t):
                     nc.tensor.matmul(
                         out=acc[:, j, :],
@@ -260,7 +254,6 @@ def tile_linearnnencoder_t_kernel(tc, x, W, b, out):
                 on(square, s - LAG_SQ_V)
             on(quant, s - LAG_QUANT)
             on(diag, s + LA_DIAG)
-            on(fold, s - LAG_ACC)
             on(xpose, s + LA_XPOSE)
             on(mx, s - LAG_QUANT)
             on(accumulate, s - LAG_ACC)

from contextlib import ExitStack

import concourse.mybir as mybir
from concourse.masks import make_identity

F32 = mybir.dt.float32
BF16 = mybir.dt.bfloat16
U32 = mybir.dt.uint32
U8 = mybir.dt.uint8
FP8X4 = mybir.dt.float8_e4m3fn_x4
ACT = mybir.ActivationFunctionType
ALU = mybir.AluOpType
AX = mybir.AxisListType

P = 128
B, T, D, O = 512, 32, 512, 128
ROWS_PP = B * T // P
SPP = ROWS_PP // T
WORDS = D // 2
UNIT = 4
NU = ROWS_PP // UNIT
UPS = T // UNIT
FLOPS = 2 * B * T * D * O
PAD_WORD = -(1.0 + 49024.0 / 8388608.0)
CHUNKS = [2, 2, 4, 4, 4] + [8] * 14

LA_TEST, LA_DIAG, LA_XPOSE = 5, 3, 2
LAG_QUANT, LAG_GELU, LAG_SQ_V, LAG_ACC = 1, 3, 4, 5
TAIL_S = 3
PER_SQ_V = 2


def evac_on_scalar(h, pr):
    return pr == 1 and h >= NU - TAIL_S


def square_on_vector(h):
    return h % PER_SQ_V == PER_SQ_V - 1 and h < NU - 2


def tile_linearnnencoder_t_kernel(tc, x, W, b, out):
    nc = tc.nc
    xv = x.flatten_outer_dims().rearrange("(p r) k -> p r k", p=P)
    ov = out.rearrange("(p j) c -> p j c", j=SPP)
    with ExitStack() as ctx:
        keep = ctx.enter_context(tc.tile_pool(name="keep", bufs=1))
        jk = ctx.enter_context(tc.tile_pool(name="jk", bufs=2))
        dgp = ctx.enter_context(tc.tile_pool(name="dgp", bufs=5))
        gp = ctx.enter_context(tc.tile_pool(name="gp", bufs=4))
        cp = ctx.enter_context(tc.tile_pool(name="cp", bufs=4))
        ys = ctx.enter_context(tc.tile_pool(name="ys", bufs=6))
        fin = ctx.enter_context(tc.tile_pool(name="fin", bufs=2))
        pacc = ctx.enter_context(tc.psum_pool(name="pacc", bufs=1))
        pxt = ctx.enter_context(tc.psum_pool(name="pxt", bufs=4))
        pmx = ctx.enter_context(tc.psum_pool(name="pmx", bufs=2))

        w_sb = keep.tile([P, D], BF16)
        zb = keep.tile([P, O], BF16)
        nc.vector.memset(zb[:], 0.0)
        where = {}
        r0 = 0
        for c, n_t in enumerate(CHUNKS):
            xc = keep.tile([P, n_t, D], BF16, name="x%d" % c)
            nc.sync.dma_start(out=xc[:], in_=xv[:, r0 : r0 + n_t, :])
            for k in range(n_t):
                where[r0 + k] = (xc, k)
            r0 += n_t
            if c == 0:
                nc.sync.dma_start(out=w_sb[:], in_=W)
                nc.sync.dma_start(out=zb[0:1, :], in_=b.rearrange("(u o) -> u o", u=1))

        ident = keep.tile([P, P], F32)
        make_identity(nc, ident[:])
        negc = keep.tile([P, 1], F32)
        nc.vector.memset(negc[:], -PAD_WORD)
        ones = keep.tile([P, P], BF16)
        nc.vector.memset(ones[:], 1.0)
        warm = keep.tile([P, 1], F32)
        nc.scalar.activation(out=warm[:], in_=negc[:], func=ACT.Gelu)

        w_w = w_sb[:].bitcast(F32)
        wt = pxt.tile([P, 2, 2, P], F32, tag="xt")
        for u in range(2):
            nc.tensor.transpose(wt[:, 0, u, :], w_w[:, u * P : (u + 1) * P], ident[:])
        gw = keep.tile([P, O, 4], BF16, align_bytes=64)
        nc.vector.tensor_copy(out=gw[:].bitcast(F32), in_=wt[:, 0, :, :].rearrange("q u o -> q o u"))
        wc = keep.tile([P, O], U32, align_bytes=64)
        wsc = keep.tile([P, O], U8, align_bytes=64)
        nc.vector.quantize_mx(out=wc[:].bitcast(FP8X4), scales=wsc[:], in_=gw[:].rearrange("q o j -> q (o j)"))

        bt = pxt.tile([P, 2, 2, P], F32, tag="xt")
        nc.tensor.matmul(out=bt[:, 0, 0, :], lhsT=ones[:], rhs=zb[:], start=True, stop=True)
        nc.tensor.matmul(out=bt[:, 1, 0, 0:64], lhsT=zb[:], rhs=ones[:, 0:64], start=True, stop=True)
        bcol = keep.tile([P, 1], F32)
        nc.vector.tensor_copy(out=bcol[:], in_=bt[:, 1, 0, 0:1])
        c0 = keep.tile([P, O], F32)
        c0sq = keep.tile([P, O], F32)

        dev = keep.tile([P, NU, 8], F32)
        vf = keep.tile([P, SPP, T], F32)
        sm = keep.tile([P, SPP, 8], F32)
        res = keep.tile([P, SPP, 2 * O], F32)
        acc_y = pacc.tile([P, SPP, O], F32)
        acc_q = pacc.tile([P, SPP, O], F32)
        dg, xt, g, codes, sc, v, y, q = {}, {}, {}, {}, {}, {}, {}, {}
        pre1, pre2 = {}, {}

        def row_words(i):
            xc, k = where[i]
            return xc[:].bitcast(F32)[:, k, :]

        def test(h):
            for a in range(UNIT):
                junk = jk.tile([P, WORDS], BF16, tag="junk")
                nc.scalar.activation(
                    out=junk[:],
                    in_=row_words(h * UNIT + a),
                    func=ACT.Square,
                    bias=negc[:],
                    scale=1.0,
                    accum_out=dev[:, h, a : a + 1],
                )

        def diag(h):
            dg[h] = dgp.tile([P, UNIT, P], F32, name="dg")
            for a in range(UNIT):
                nc.vector.tensor_scalar(
                    out=dg[h][:, a, :],
                    in0=ident[:],
                    scalar1=dev[:, h, a : a + 1],
                    scalar2=0.0,
                    op0=ALU.mult,
                    op1=ALU.is_gt,
                )

        def xpose(h):
            for pr in range(2):
                xt[h, pr] = pxt.tile([P, 2, 2, P], F32, name="xt")
                for a in range(2):
                    rw = row_words(h * UNIT + 2 * pr + a)
                    for u in range(2):
                        nc.tensor.transpose(xt[h, pr][:, a, u, :], rw[:, u * P : (u + 1) * P], dg[h][:, 2 * pr + a, :])

        def evac(h):
            g[h] = gp.tile([P, UNIT * P, 4], BF16, name="g", align_bytes=64)
            g_w = g[h][:].bitcast(F32)
            for pr in range(2):
                dst = g_w[:, 2 * pr * P : (2 * pr + 2) * P, :].rearrange("q (a t) u -> q a t u", a=2)
                src = xt[h, pr][:].rearrange("q a u t -> q a t u")
                if evac_on_scalar(h, pr):
                    nc.scalar.copy(out=dst, in_=src)
                else:
                    nc.vector.tensor_copy(out=dst, in_=src)

        def quant(h):
            codes[h] = cp.tile([P, UNIT * P], U32, name="codes", align_bytes=64)
            sc[h] = cp.tile([P, UNIT * P], U8, name="sc", align_bytes=64)
            nc.vector.quantize_mx(
                out=codes[h][:].bitcast(FP8X4), scales=sc[h][:], in_=g[h][:].rearrange("q t j -> q (t j)")
            )

        def mx(h):
            v[h] = pmx.tile([P, UNIT * P], F32, name="v")
            nc.tensor.matmul_mx(
                out=v[h][:],
                lhsT=wc[:].bitcast(FP8X4),
                lhsT_scale=wsc[:],
                rhs=codes[h][:].bitcast(FP8X4),
                rhs_scale=sc[h][:],
                start=True,
                stop=True,
            )

        def gelu(h):
            y[h] = ys.tile([P, UNIT * P], F32, name="y")
            nc.scalar.activation(out=y[h][:], in_=v[h][:], func=ACT.Gelu, bias=bcol[:], scale=1.0)

        def square(h):
            q[h] = ys.tile([P, UNIT * P], F32, name="q")
            if square_on_vector(h):
                nc.vector.tensor_tensor(out=q[h][:], in0=y[h][:], in1=y[h][:], op=ALU.mult)
            else:
                nc.scalar.activation(out=q[h][:], in_=y[h][:], func=ACT.Square)

        def accumulate(h):
            j = h // UPS
            for src, acc, n_t in ((y, acc_y, UNIT), (q, acc_q, UNIT)):
                for a in range(n_t):
                    nc.tensor.matmul(
                        out=acc[:, j, :],
                        lhsT=src[h][:, a * P : (a + 1) * P],
                        rhs=ident[:],
                        is_transpose=True,
                        start=(h % UPS == 0 and a == 0),
                        stop=(h % UPS == UPS - 1 and a == n_t - 1),
                    )

        def counts(j):
            nc.vector.tensor_scalar(
                out=vf[:, j, :].rearrange("p (h a) -> p h a", a=UNIT),
                in0=dev[:, j * UPS : (j + 1) * UPS, 0:UNIT],
                scalar1=0.0,
                scalar2=None,
                op0=ALU.is_gt,
            )
            n = sm[:, j, 0:1]
            nc.vector.tensor_reduce(out=n, in_=vf[:, j, :], axis=AX.X, op=ALU.add)
            nc.vector.tensor_scalar(out=sm[:, j, 1:2], in0=n, scalar1=-float(T), scalar2=None, op0=ALU.add)
            nc.vector.tensor_scalar(out=sm[:, j, 2:3], in0=n, scalar1=1.0, scalar2=None, op0=ALU.max)
            nc.vector.tensor_scalar(out=sm[:, j, 3:4], in0=n, scalar1=-1.0, scalar2=1.0, op0=ALU.add, op1=ALU.max)
            nc.vector.reciprocal(out=sm[:, j, 4:6], in_=sm[:, j, 2:4])
            nc.vector.scalar_tensor_tensor(
                out=sm[:, j, 6:7], in0=n, scalar=0.0, in1=sm[:, j, 4:5], op0=ALU.is_gt, op1=ALU.mult
            )
            nc.vector.scalar_tensor_tensor(
                out=sm[:, j, 7:8], in0=n, scalar=1.0, in1=sm[:, j, 5:6], op0=ALU.is_gt, op1=ALU.mult
            )
            pre1[j] = fin.tile([P, O], F32, name="pre1")
            nc.vector.tensor_scalar(out=pre1[j][:], in0=c0[:], scalar1=sm[:, j, 1:2], scalar2=None, op0=ALU.mult)
            pre2[j] = fin.tile([P, O], F32, name="pre2")
            nc.vector.tensor_scalar(out=pre2[j][:], in0=c0sq[:], scalar1=sm[:, j, 1:2], scalar2=None, op0=ALU.mult)

        def finish_mean(j):
            s1 = fin.tile([P, O], F32, name="s1")
            nc.vector.tensor_tensor(out=s1[:], in0=pre1[j][:], in1=acc_y[:, j, :], op=ALU.add)
            nc.vector.tensor_scalar(
                out=res[:, j, O : 2 * O], in0=s1[:], scalar1=sm[:, j, 6:7], scalar2=None, op0=ALU.mult
            )
            tt = fin.tile([P, O], F32, name="tt")
            nc.vector.tensor_tensor(out=tt[:], in0=res[:, j, O : 2 * O], in1=s1[:], op=ALU.mult)
            nc.vector.tensor_tensor(out=pre2[j][:], in0=pre2[j][:], in1=tt[:], op=ALU.subtract)

        def finish_var(j):
            d = fin.tile([P, O], F32, name="d")
            nc.vector.tensor_tensor(out=d[:], in0=pre2[j][:], in1=acc_q[:, j, :], op=ALU.add)
            nc.vector.tensor_scalar(
                out=res[:, j, 0:O], in0=d[:], scalar1=sm[:, j, 7:8], scalar2=1e-30, op0=ALU.mult, op1=ALU.max
            )

        def on(stage, h):
            if 0 <= h < NU:
                stage(h)

        for s in range(-LA_TEST, NU + LAG_ACC + 3):
            on(evac, s)
            on(gelu, s - LAG_GELU)
            if not square_on_vector(s - LAG_GELU):
                on(square, s - LAG_GELU)
            on(test, s + LA_TEST)
            if s == -LA_TEST:
                nc.scalar.activation(out=c0[:], in_=bt[:, 0, 0, :], func=ACT.Gelu)
                nc.scalar.activation(out=c0sq[:], in_=c0[:], func=ACT.Square)
            if square_on_vector(s - LAG_SQ_V):
                on(square, s - LAG_SQ_V)
            on(quant, s - LAG_QUANT)
            on(diag, s + LA_DIAG)
            on(xpose, s + LA_XPOSE)
            on(mx, s - LAG_QUANT)
            on(accumulate, s - LAG_ACC)
            last = s + LA_DIAG
            if 0 <= last < NU and last % UPS == UPS - 1:
                counts(last // UPS)
            for j in range(SPP):
                lag = 2 if j < SPP - 1 else 0
                if s - LAG_ACC - lag == j * UPS + UPS - 1:
                    finish_mean(j)
                    finish_var(j)
        nc.scalar.activation(out=res[:, 0 : SPP - 1, 0:O], in_=res[:, 0 : SPP - 1, 0:O], func=ACT.Sqrt)
        nc.sync.dma_start(out=ov[:, 0 : SPP - 1, :], in_=res[:, 0 : SPP - 1, :])
        nc.scalar.activation(out=res[:, SPP - 1, 0:O], in_=res[:, SPP - 1, 0:O], func=ACT.Sqrt)
        nc.sync.dma_start(out=ov[:, SPP - 1, :], in_=res[:, SPP - 1, :])
